import numpy as np
import ml_dtypes


def mxq(x, axis, fmt="e4m3"):
    dtype, down = {"e4m3": (ml_dtypes.float8_e4m3fn, 7), "e5m2": (ml_dtypes.float8_e5m2, 14)}[fmt]
    v = np.moveaxis(np.asarray(x, np.float32).astype(ml_dtypes.bfloat16).astype(np.float64), axis, -1)
    blocks = v.reshape(v.shape[:-1] + (-1, 32))
    amax = np.abs(blocks).max(-1, keepdims=True)
    byte = np.maximum(np.where(amax > 0, np.frexp(amax)[1] - 1 + 127, 0) - down, 1)
    scale = np.exp2(byte - 127.0)
    codes = (blocks / scale).astype(np.float32).astype(dtype).astype(np.float64)
    return np.moveaxis((codes * scale).reshape(v.shape), -1, axis)


WIDE = False


def mx_kscale(k):
    if not WIDE:
        return np.ones(k)
    levels = np.array([10, -10, 5, -5, 0])
    if k % 512:
        return np.exp2(np.random.permutation(np.resize(levels, k // 32))).repeat(32)
    a = np.empty((k // 512, 16))
    for p in range(k // 512):
        a[p, :8] = np.random.permutation(np.resize(levels, 8))
        for g in range(8):
            far = levels[np.abs(levels - a[p, g]) >= 10]
            a[p, g + 8] = far[np.random.randint(len(far))]
    return np.exp2(a.ravel()).repeat(32)


BF16 = ml_dtypes.bfloat16


def bf(x):
    return np.asarray(x, np.float32).astype(BF16)


def f64(x):
    return np.asarray(x).astype(np.float64)


B, S, IN_DIM, OUT_DIM, MOD_DIM = 4, 512, 512, 512, 512
EPS = 1e-8
GAIN = np.sqrt(2.0 / (1.0 + 0.2 ** 2))


def setup_inputs():
    ks = mx_kscale(MOD_DIM)
    kt = mx_kscale(IN_DIM)
    return {"x": bf(np.random.standard_normal((B, S, IN_DIM))),
            "modulation": bf(np.random.standard_normal((B, S, MOD_DIM)) * ks),
            "weight": bf(np.random.standard_normal((OUT_DIM, IN_DIM)) * GAIN / np.sqrt(IN_DIM) / kt[None, :]),
            "bias": bf(np.random.standard_normal(OUT_DIM) * 0.1),
            "mod_w": bf(np.random.standard_normal((IN_DIM, MOD_DIM)) / np.sqrt(MOD_DIM) * kt[:, None] / ks[None, :]),
            "mod_b": bf((1.0 + 0.1 * np.random.standard_normal(IN_DIM)) * kt)}


def reference(x, modulation, weight, bias, mod_w, mod_b):
    xf, w = f64(x), f64(weight)
    s = f64(bf(mxq(f64(modulation), 2, "e4m3") @ mxq(f64(mod_w), 1, "e4m3").T)) + f64(mod_b)
    out = mxq(xf * s, 2, "e4m3") @ mxq(w, 1, "e4m3").T
    demod = 1.0 / np.sqrt((mxq(s * s, 2, "e4m3") @ mxq(w * w, 1, "e4m3").T) + EPS)
    return out * demod + f64(bias)

@@ -1,0 +1,279 @@
+from contextlib import ExitStack
+
+import concourse.mybir as mybir
+from concourse.masks import make_identity
+
+F32 = mybir.dt.float32
+BF16 = mybir.dt.bfloat16
+U32 = mybir.dt.uint32
+U8 = mybir.dt.uint8
+FP8X4 = mybir.dt.float8_e4m3fn_x4
+ACT = mybir.ActivationFunctionType
+ALU = mybir.AluOpType
+
+P = 128
+D = 512
+CHUNKS = 4
+UNITS = 8
+UNIT = 256
+RUN = 4
+EPS = 1e-8
+FLOPS = 3 * 2 * CHUNKS * D * D * D
+S1_DTYPE = BF16
+
+
+def tile_modulatedlinear_kernel(tc, x, modulation, weight, bias, mod_w, mod_b, out):
+    nc = tc.nc
+    with ExitStack() as ctx:
+        const = ctx.enter_context(tc.tile_pool(name="const", bufs=1))
+        rows = ctx.enter_context(tc.tile_pool(name="rows", bufs=1))
+        work = ctx.enter_context(tc.tile_pool(name="work", bufs=2))
+        psum = ctx.enter_context(tc.psum_pool(name="psum", bufs=1))
+        ctx.enter_context(tc.manual_schedule())
+
+        def unit_view(tensor, u):
+            return tensor[u // 2].rearrange("(r c) k -> r c k", c=4)[:, 2 * (u % 2):2 * (u % 2) + 2, :]
+
+        def load(view, name):
+            t = rows.tile([P, 2, D], BF16, name=name)
+            nc.sync.dma_start(out=t[:], in_=view)
+            return t
+
+        ident = const.tile([P, P], F32, name="ident")
+        make_identity(nc, ident[:])
+        ident_bf = const.tile([P, P], BF16, name="ident_bf")
+        make_identity(nc, ident_bf[:])
+        one = const.tile([P, 1], F32, name="one")
+        nc.vector.memset(one[:], 1.0)
+        warm = const.tile([P, 1], F32, name="warm")
+        modb_bf = const.tile([P, 4], BF16, name="modb_bf")
+        nc.scalar.dma_start(out=modb_bf[:], in_=mod_b.rearrange("(p j) -> p j", j=4))
+        bias_row = const.tile([P, D], BF16, name="bias_row")
+        nc.gpsimd.memset(bias_row[:], 0.0)
+        nc.scalar.activation(out=warm[:], in_=one[:], func=ACT.Abs_reciprocal_sqrt, bias=EPS, scale=1.0)
+        ones = const.tile([P, P], BF16, name="ones")
+        nc.gpsimd.memset(ones[:], 1.0)
+        nc.gpsimd.dma_start(out=bias_row[0:1, :], in_=bias.rearrange("(a n) -> a n", a=1))
+
+        mw_view = mod_w.rearrange("(r c) k -> r c k", c=4)
+        w_view = weight.rearrange("(c r) k -> r c k", c=4)
+        m_rows, x_rows = {}, {}
+        m_rows[0] = load(unit_view(modulation, 0), "m0")
+        m_rows[1] = load(unit_view(modulation, 1), "m1")
+        mw_rows = [load(mw_view[:, 0:2, :], "mw0"), load(mw_view[:, 2:4, :], "mw1")]
+        w_rows = [load(w_view[:, 0:2, :], "w0"), load(w_view[:, 2:4, :], "w1")]
+        x_rows[0] = load(unit_view(x, 0), "x0")
+        m_rows[2] = load(unit_view(modulation, 2), "m2")
+        m_rows[3] = load(unit_view(modulation, 3), "m3")
+        x_rows[1] = load(unit_view(x, 1), "x1")
+        for u in range(2, UNITS):
+            if u + 2 < UNITS:
+                m_rows[u + 2] = load(unit_view(modulation, u + 2), "m%d" % (u + 2))
+            x_rows[u] = load(unit_view(x, u), "x%d" % u)
+
+        modb = const.tile([P, 4], F32, name="modb")
+        nc.vector.tensor_copy(out=modb[:], in_=modb_bf[:])
+
+        def operand(pool, name, bufs):
+            return (pool.tile([P, 4 * D], BF16, tag=name + "_v", name=name + "_v", bufs=bufs, align_bytes=64),
+                    pool.tile([P, D], U32, tag=name + "_c", name=name + "_c", bufs=bufs, align_bytes=64),
+                    pool.tile([P, D], U8, tag=name + "_s", name=name + "_s", bufs=bufs, align_bytes=64))
+
+        def values(op, h):
+            return op[0][:, 4 * UNIT * h:4 * UNIT * (h + 1)]
+
+        def quantize(op, lo, hi):
+            nc.vector.quantize_mx(out=op[1][:, lo:hi].bitcast(FP8X4), scales=op[2][:, lo:hi], in_=op[0][:, 4 * lo:4 * hi])
+
+        def matmul_mx(acc, a, a0, b):
+            nc.tensor.matmul_mx(out=acc[:], lhsT=a[1][:, a0:a0 + P].bitcast(FP8X4), lhsT_scale=a[2][:, a0:a0 + P],
+                                rhs=b[1][:].bitcast(FP8X4), rhs_scale=b[2][:], start=True, stop=True)
+
+        def word_transposes(src, tag, bufs=1):
+            bank = psum.tile([P, 2, UNIT], F32, tag=tag, bufs=bufs, name="t_" + tag)
+            for c in range(2):
+                words = src[:, c, :].bitcast(F32)
+                for h in range(2):
+                    nc.tensor.transpose(bank[:, h, c * P:(c + 1) * P], words[:, h:UNIT:2], ident[:])
+            return bank
+
+        def copy_out(copy, bank, dst):
+            copy(out=dst.bitcast(F32).rearrange("p (n h) -> p n h", h=2), in_=bank[:].rearrange("p h n -> p n h"))
+
+        mw = operand(const, "mw", 1)
+        w = operand(const, "w", 1)
+        w2 = operand(const, "w2", 1)
+        bias_sb = const.tile([P, D], F32, name="bias_sb")
+        bias_bank = []
+        m_bank, x_bank, m_op, s1_bank, s_sb, a_op, y_bank, q_bank, d_sb, yd_sb, res_sb = {}, {}, {}, {}, {}, {}, {}, {}, {}, {}, {}
+
+        def mod_transposes(k, tag="tm", bufs=1):
+            m_bank[k] = word_transposes(m_rows[k], tag, bufs)
+
+        def mod_copy(k, copy):
+            if k % 2 == 0:
+                m_op[k // 2] = operand(work, "m", 2)
+            copy_out(copy, m_bank[k], values(m_op[k // 2], k % 2))
+
+        def stage1(g, j):
+            s1_bank[g, j] = psum.tile([P, D], S1_DTYPE, tag="s1", bufs=2, name="s1")
+            matmul_mx(s1_bank[g, j], mw, P * j, m_op[g])
+
+        def add_mod_b(g, j, on_vector=False):
+            if j == 0:
+                s_sb[g] = work.tile([P, 4, D], F32, tag="s", name="s", bufs=2)
+            if on_vector:
+                nc.vector.tensor_scalar(out=s_sb[g][:, j, :], in0=s1_bank[g, j][:], scalar1=modb[:, j:j + 1], scalar2=None, op0=ALU.add)
+            else:
+                nc.scalar.activation(out=s_sb[g][:, j, :], in_=s1_bank[g, j][:], func=ACT.Identity, bias=modb[:, j:j + 1], scale=1.0)
+
+        def x_transposes(u):
+            x_bank[u] = psum.tile([P, 4, UNIT], BF16, tag="tx", bufs=1, name="t_x")
+            for c in range(2):
+                for j in range(4):
+                    nc.tensor.transpose(x_bank[u][:, j, c * P:(c + 1) * P], x_rows[u][:, c, j:D:4], ident_bf[:])
+
+        def s_of(u):
+            return s_sb[u // 2][:, :, UNIT * (u % 2):UNIT * (u % 2 + 1)]
+
+        def s_times_s(u):
+            a_op[u] = operand(work, "a", 2)
+            nc.scalar.activation(out=values(a_op[u], 1).rearrange("p (c i j) -> p c j i", i=RUN, j=4),
+                                 in_=s_of(u).rearrange("p j (c i) -> p c j i", i=RUN), func=ACT.Square)
+
+        def x_times_s(u):
+            nc.vector.tensor_tensor(out=values(a_op[u], 0).rearrange("p (c i j) -> p c j i", i=RUN, j=4),
+                                    in0=s_of(u).rearrange("p j (c i) -> p c j i", i=RUN),
+                                    in1=x_bank[u][:].rearrange("p j (c i) -> p c j i", i=RUN), op=ALU.mult)
+
+        def stage2(u, c):
+            y_bank[u, c] = psum.tile([P, D], F32, tag="y", bufs=2, name="y")
+            matmul_mx(y_bank[u, c], a_op[u], P * c, w)
+
+        def stage3(u, c):
+            q_bank[u, c] = psum.tile([P, D], F32, tag="q", bufs=2, name="q")
+            matmul_mx(q_bank[u, c], a_op[u], UNIT + P * c, w2)
+
+        def demod(u, c):
+            d_sb[u, c] = work.tile([P, D], F32, tag="d", name="d", bufs=4)
+            nc.scalar.activation(out=d_sb[u, c][:], in_=q_bank[u, c][:], func=ACT.Abs_reciprocal_sqrt, bias=EPS, scale=1.0)
+
+        def y_times_d(u, c):
+            yd_sb[u, c] = work.tile([P, D], F32, tag="yd", name="yd", bufs=3)
+            nc.vector.tensor_tensor(out=yd_sb[u, c][:], in0=y_bank[u, c][:], in1=d_sb[u, c][:], op=ALU.mult)
+
+        def spread_bias(tag, bufs):
+            bank = psum.tile([P, D], F32, tag=tag, bufs=bufs, name="bias_bank")
+            nc.tensor.matmul(out=bank[:], lhsT=ones[:], rhs=bias_row[:], start=True, stop=True)
+            bias_bank.append(bank)
+
+        def add_bias_gpsimd(u, c):
+            res_sb[u, c] = work.tile([P, D], F32, tag="res", name="res", bufs=4)
+            nc.gpsimd.tensor_tensor(out=res_sb[u, c][:], in0=yd_sb[u, c][:], in1=bias_sb[:], op=ALU.add)
+
+        def add_bias_vector(u, c, bias_tile):
+            res_sb[u, c] = work.tile([P, D], F32, tag="res", name="res", bufs=4)
+            nc.vector.tensor_tensor(out=res_sb[u, c][:], in0=yd_sb[u, c][:], in1=bias_tile[:], op=ALU.add)
+
+        def store(u, c):
+            nc.sync.dma_start(out=unit_view(out, u)[:, c, :], in_=res_sb[u, c][:])
+
+        mod_transposes(0, "y", 2)
+        mod_transposes(1, "q", 2)
+        mw_bank = [word_transposes(mw_rows[0], "y", 2), word_transposes(mw_rows[1], "q", 2)]
+        w_bank = [word_transposes(w_rows[0], "tm")]
+        mod_copy(0, nc.scalar.copy)
+        mod_copy(1, nc.vector.tensor_copy)
+        copy_out(nc.scalar.copy, mw_bank[0], values(mw, 0))
+        quantize(m_op[0], 0, UNIT)
+        quantize(m_op[0], UNIT, D)
+        quantize(mw, 0, UNIT)
+        copy_out(nc.scalar.copy, mw_bank[1], values(mw, 1))
+        stage1(0, 0)
+        stage1(0, 1)
+        w_bank.append(word_transposes(w_rows[1], "y", 2))
+        quantize(mw, UNIT, D)
+        copy_out(nc.scalar.copy, w_bank[0], values(w, 0))
+        add_mod_b(0, 0)
+        add_mod_b(0, 1, on_vector=True)
+        stage1(0, 2)
+        stage1(0, 3)
+        x_transposes(0)
+        copy_out(nc.scalar.copy, w_bank[1], values(w, 1))
+        quantize(w, 0, UNIT)
+        quantize(w, UNIT, D)
+        add_mod_b(0, 2)
+        add_mod_b(0, 3, on_vector=True)
+        mod_transposes(2, "q", 2)
+        mod_transposes(3, "y", 2)
+        spread_bias("y", 2)
+        mod_transposes(4)
+
+        for u in range(UNITS):
+            g = u // 2
+            if u == 1:
+                nc.scalar.copy(out=bias_sb[:], in_=bias_bank[0][:])
+                mod_copy(4, nc.vector.tensor_copy)
+                mod_transposes(5)
+            if u == 4:
+                spread_bias("tm", 1)
+            if u >= 2:
+                y_times_d(u - 2, 0)
+                add_bias_gpsimd(u - 2, 0)
+                store(u - 2, 0)
+            if u >= 1:
+                stage2(u - 1, 0)
+            if u >= 2:
+                y_times_d(u - 2, 1)
+            if u >= 1:
+                stage2(u - 1, 1)
+            s_times_s(u)
+            x_times_s(u)
+            if u == 1:
+                mod_copy(5, nc.vector.tensor_copy)
+            if u == 2 or u == 3:
+                mod_copy(u + 4, nc.scalar.copy)
+            if u >= 1:
+                demod(u - 1, 0)
+                demod(u - 1, 1)
+            if u == 0:
+                mod_copy(2, nc.scalar.copy)
+                mod_copy(3, nc.vector.tensor_copy)
+                nc.scalar.activation(out=values(w2, 0), in_=values(w, 0), func=ACT.Square)
+                nc.vector.tensor_tensor(out=values(w2, 1), in0=values(w, 1), in1=values(w, 1), op=ALU.mult)
+                quantize(m_op[1], 0, D)
+                quantize(w2, 0, D)
+            if g + 1 < CHUNKS:
+                stage1(g + 1, 2 * (u % 2))
+                stage1(g + 1, 2 * (u % 2) + 1)
+                add_mod_b(g + 1, 2 * (u % 2))
+                add_mod_b(g + 1, 2 * (u % 2) + 1)
+            if u == 1 or u == 2:
+                mod_transposes(u + 5)
+            if u + 1 < UNITS:
+                x_transposes(u + 1)
+            if u >= 2:
+                add_bias_vector(u - 2, 1, bias_sb if u < 4 else bias_bank[1])
+                store(u - 2, 1)
+            quantize(a_op[u], 0, D)
+            stage3(u, 0)
+            stage3(u, 1)
+            if u == 1 or u == 3:
+                quantize(m_op[(u + 3) // 2], 0, D)
+
+        y_times_d(6, 0)
+        add_bias_gpsimd(6, 0)
+        store(6, 0)
+        stage2(7, 0)
+        y_times_d(6, 1)
+        add_bias_gpsimd(6, 1)
+        stage2(7, 1)
+        demod(7, 0)
+        demod(7, 1)
+        y_times_d(7, 0)
+        add_bias_vector(7, 0, bias_bank[1])
+        store(7, 0)
+        y_times_d(7, 1)
+        store(6, 1)
+        add_bias_vector(7, 1, bias_bank[1])
+        store(7, 1)

@@ -131,7 +131,7 @@ def tile_modulatedlinear_kernel(tc, x, modulation, weight, bias, mod_w, mod_b, o
             x_bank[u] = psum.tile([P, 4, UNIT], BF16, tag="tx", bufs=1, name="t_x")
             for c in range(2):
                 for j in range(4):
-                    nc.tensor.transpose(x_bank[u][:, j, c * P:(c + 1) * P], x_rows[u][:, c, j:D:4], ident_bf[:])
+                    nc.tensor.matmul(out=x_bank[u][:, j, c * P:(c + 1) * P], lhsT=x_rows[u][:, c, j:D:4], rhs=ident_bf[:], start=True, stop=True)
 
         def s_of(u):
             return s_sb[u // 2][:, :, UNIT * (u % 2):UNIT * (u % 2 + 1)]

@@ -159,7 +159,7 @@ def tile_modulatedlinear_kernel(tc, x, modulation, weight, bias, mod_w, mod_b, o
             nc.scalar.activation(out=d_sb[u, c][:], in_=q_bank[u, c][:], func=ACT.Abs_reciprocal_sqrt, bias=EPS, scale=1.0)
 
         def y_times_d(u, c):
-            yd_sb[u, c] = work.tile([P, D], F32, tag="yd", name="yd", bufs=3)
+            yd_sb[u, c] = work.tile([P, D], F32, tag="yd", name="yd", bufs=6)
             nc.vector.tensor_tensor(out=yd_sb[u, c][:], in0=y_bank[u, c][:], in1=d_sb[u, c][:], op=ALU.mult)
 
         def spread_bias(tag, bufs):
@@ -168,11 +168,11 @@ def tile_modulatedlinear_kernel(tc, x, modulation, weight, bias, mod_w, mod_b, o
             bias_bank.append(bank)
 
         def add_bias_gpsimd(u, c):
-            res_sb[u, c] = work.tile([P, D], F32, tag="res", name="res", bufs=4)
+            res_sb[u, c] = work.tile([P, D], F32, tag="res", name="res", bufs=8)
             nc.gpsimd.tensor_tensor(out=res_sb[u, c][:], in0=yd_sb[u, c][:], in1=bias_sb[:], op=ALU.add)
 
         def add_bias_vector(u, c, bias_tile):
-            res_sb[u, c] = work.tile([P, D], F32, tag="res", name="res", bufs=4)
+            res_sb[u, c] = work.tile([P, D], F32, tag="res", name="res", bufs=8)
             nc.vector.tensor_tensor(out=res_sb[u, c][:], in0=yd_sb[u, c][:], in1=bias_tile[:], op=ALU.add)
 
         def store(u, c):
@@ -211,6 +211,24 @@ def tile_modulatedlinear_kernel(tc, x, modulation, weight, bias, mod_w, mod_b, o
 
         for u in range(UNITS):
             g = u // 2
+            if u == 0:
+                s_times_s(0)
+                x_times_s(0)
+                mod_copy(2, nc.scalar.copy)
+                mod_copy(3, nc.vector.tensor_copy)
+                nc.scalar.activation(out=values(w2, 0), in_=values(w, 0), func=ACT.Square)
+                nc.vector.tensor_tensor(out=values(w2, 1), in0=values(w, 1), in1=values(w, 1), op=ALU.mult)
+                quantize(m_op[1], 0, D)
+                quantize(w2, 0, D)
+                stage1(1, 0)
+                stage1(1, 1)
+                add_mod_b(1, 0)
+                add_mod_b(1, 1)
+                x_transposes(1)
+                quantize(a_op[0], 0, D)
+                stage3(0, 0)
+                stage3(0, 1)
+                continue
             if u == 1:
                 nc.scalar.copy(out=bias_sb[:], in_=bias_bank[0][:])
                 mod_copy(4, nc.vector.tensor_copy)
@@ -221,45 +239,33 @@ def tile_modulatedlinear_kernel(tc, x, modulation, weight, bias, mod_w, mod_b, o
                 y_times_d(u - 2, 0)
                 add_bias_gpsimd(u - 2, 0)
                 store(u - 2, 0)
-            if u >= 1:
-                stage2(u - 1, 0)
-            if u >= 2:
-                y_times_d(u - 2, 1)
-            if u >= 1:
-                stage2(u - 1, 1)
-            s_times_s(u)
-            x_times_s(u)
-            if u == 1:
-                mod_copy(5, nc.vector.tensor_copy)
-            if u == 2 or u == 3:
-                mod_copy(u + 4, nc.scalar.copy)
-            if u >= 1:
-                demod(u - 1, 0)
-                demod(u - 1, 1)
-            if u == 0:
-                mod_copy(2, nc.scalar.copy)
-                mod_copy(3, nc.vector.tensor_copy)
-                nc.scalar.activation(out=values(w2, 0), in_=values(w, 0), func=ACT.Square)
-                nc.vector.tensor_tensor(out=values(w2, 1), in0=values(w, 1), in1=values(w, 1), op=ALU.mult)
-                quantize(m_op[1], 0, D)
-                quantize(w2, 0, D)
+            if u == 2 or u == 4:
+                quantize(m_op[u // 2 + 1], 0, D)
+            stage2(u - 1, 0)
             if g + 1 < CHUNKS:
                 stage1(g + 1, 2 * (u % 2))
                 stage1(g + 1, 2 * (u % 2) + 1)
-                add_mod_b(g + 1, 2 * (u % 2))
-                add_mod_b(g + 1, 2 * (u % 2) + 1)
-            if u == 1 or u == 2:
-                mod_transposes(u + 5)
+            s_times_s(u)
+            x_times_s(u)
+            if u <= 3:
+                mod_copy(u + 4, nc.vector.tensor_copy)
             if u + 1 < UNITS:
                 x_transposes(u + 1)
+            if u == 1 or u == 2:
+                mod_transposes(u + 5)
             if u >= 2:
-                add_bias_vector(u - 2, 1, bias_sb if u < 4 else bias_bank[1])
+                y_times_d(u - 2, 1)
+                add_bias_gpsimd(u - 2, 1)
                 store(u - 2, 1)
+            stage2(u - 1, 1)
+            demod(u - 1, 0)
+            demod(u - 1, 1)
+            if g + 1 < CHUNKS:
+                add_mod_b(g + 1, 2 * (u % 2))
+                add_mod_b(g + 1, 2 * (u % 2) + 1)
             quantize(a_op[u], 0, D)
             stage3(u, 0)
             stage3(u, 1)
-            if u == 1 or u == 3:
-                quantize(m_op[(u + 3) // 2], 0, D)
 
         y_times_d(6, 0)
         add_bias_gpsimd(6, 0)

@@ -239,16 +239,18 @@ def tile_modulatedlinear_kernel(tc, x, modulation, weight, bias, mod_w, mod_b, o
                 y_times_d(u - 2, 0)
                 add_bias_gpsimd(u - 2, 0)
                 store(u - 2, 0)
-            if u == 2 or u == 4:
-                quantize(m_op[u // 2 + 1], 0, D)
             stage2(u - 1, 0)
             if g + 1 < CHUNKS:
                 stage1(g + 1, 2 * (u % 2))
                 stage1(g + 1, 2 * (u % 2) + 1)
+            if u == 3:
+                mod_copy(7, nc.vector.tensor_copy)
             s_times_s(u)
             x_times_s(u)
-            if u <= 3:
+            if u <= 2:
                 mod_copy(u + 4, nc.vector.tensor_copy)
+            if u == 3:
+                quantize(m_op[3], 0, D)
             if u + 1 < UNITS:
                 x_transposes(u + 1)
             if u == 1 or u == 2:
@@ -266,6 +268,8 @@ def tile_modulatedlinear_kernel(tc, x, modulation, weight, bias, mod_w, mod_b, o
             quantize(a_op[u], 0, D)
             stage3(u, 0)
             stage3(u, 1)
+            if u == 1:
+                quantize(m_op[2], 0, D)
 
         y_times_d(6, 0)
         add_bias_gpsimd(6, 0)

@@ -55,6 +55,16 @@ def tile_modulatedlinear_kernel(tc, x, modulation, weight, bias, mod_w, mod_b, o
         nc.gpsimd.memset(ones[:], 1.0)
         nc.gpsimd.dma_start(out=bias_row[0:1, :], in_=bias.rearrange("(a n) -> a n", a=1))
 
+        zeros = const.tile([P, UNIT], F32, name="zeros")
+        nc.vector.memset(zeros[:], 0.0)
+
+        def idle_matmul():
+            idle_bank = psum.tile([P, UNIT], F32, tag="s1", bufs=2, name="idle_bank")
+            nc.tensor.matmul(out=idle_bank[:], lhsT=zeros[:, 0:P], rhs=zeros[:], start=True, stop=True)
+
+        for i in range(3):
+            idle_matmul()
+
         mw_view = mod_w.rearrange("(r c) k -> r c k", c=4)
         w_view = weight.rearrange("(c r) k -> r c k", c=4)
         m_rows, x_rows = {}, {}
@@ -70,6 +80,9 @@ def tile_modulatedlinear_kernel(tc, x, modulation, weight, bias, mod_w, mod_b, o
             if u + 2 < UNITS:
                 m_rows[u + 2] = load(unit_view(modulation, u + 2), "m%d" % (u + 2))
             x_rows[u] = load(unit_view(x, u), "x%d" % u)
+
+        bias_bf = const.tile([P, D], BF16, name="bias_bf")
+        nc.sync.dma_start(out=bias_bf[:], in_=bias.partition_broadcast(P))
 
         modb = const.tile([P, 4], F32, name="modb")
         nc.vector.tensor_copy(out=modb[:], in_=modb_bf[:])
@@ -103,7 +116,6 @@ def tile_modulatedlinear_kernel(tc, x, modulation, weight, bias, mod_w, mod_b, o
         mw = operand(const, "mw", 1)
         w = operand(const, "w", 1)
         w2 = operand(const, "w2", 1)
-        bias_sb = const.tile([P, D], F32, name="bias_sb")
         bias_bank = []
         m_bank, x_bank, m_op, s1_bank, s_sb, a_op, y_bank, q_bank, d_sb, yd_sb, res_sb = {}, {}, {}, {}, {}, {}, {}, {}, {}, {}, {}
 
@@ -169,7 +181,7 @@ def tile_modulatedlinear_kernel(tc, x, modulation, weight, bias, mod_w, mod_b, o
 
         def add_bias_gpsimd(u, c):
             res_sb[u, c] = work.tile([P, D], F32, tag="res", name="res", bufs=8)
-            nc.gpsimd.tensor_tensor(out=res_sb[u, c][:], in0=yd_sb[u, c][:], in1=bias_sb[:], op=ALU.add)
+            nc.gpsimd.tensor_tensor(out=res_sb[u, c][:], in0=yd_sb[u, c][:], in1=bias_bf[:], op=ALU.add)
 
         def add_bias_vector(u, c, bias_tile):
             res_sb[u, c] = work.tile([P, D], F32, tag="res", name="res", bufs=8)
@@ -180,6 +192,7 @@ def tile_modulatedlinear_kernel(tc, x, modulation, weight, bias, mod_w, mod_b, o
 
         mod_transposes(0, "y", 2)
         mod_transposes(1, "q", 2)
+        idle_matmul()
         mw_bank = [word_transposes(mw_rows[0], "y", 2), word_transposes(mw_rows[1], "q", 2)]
         w_bank = [word_transposes(w_rows[0], "tm")]
         mod_copy(0, nc.scalar.copy)
@@ -206,7 +219,6 @@ def tile_modulatedlinear_kernel(tc, x, modulation, weight, bias, mod_w, mod_b, o
         add_mod_b(0, 3, on_vector=True)
         mod_transposes(2, "q", 2)
         mod_transposes(3, "y", 2)
-        spread_bias("y", 2)
         mod_transposes(4)
 
         for u in range(UNITS):
@@ -220,17 +232,16 @@ def tile_modulatedlinear_kernel(tc, x, modulation, weight, bias, mod_w, mod_b, o
                 nc.vector.tensor_tensor(out=values(w2, 1), in0=values(w, 1), in1=values(w, 1), op=ALU.mult)
                 quantize(m_op[1], 0, D)
                 quantize(w2, 0, D)
+                x_transposes(1)
                 stage1(1, 0)
                 stage1(1, 1)
                 add_mod_b(1, 0)
                 add_mod_b(1, 1)
-                x_transposes(1)
                 quantize(a_op[0], 0, D)
                 stage3(0, 0)
                 stage3(0, 1)
                 continue
             if u == 1:
-                nc.scalar.copy(out=bias_sb[:], in_=bias_bank[0][:])
                 mod_copy(4, nc.vector.tensor_copy)
                 mod_transposes(5)
             if u == 4:
@@ -281,9 +292,9 @@ def tile_modulatedlinear_kernel(tc, x, modulation, weight, bias, mod_w, mod_b, o
         demod(7, 0)
         demod(7, 1)
         y_times_d(7, 0)
-        add_bias_vector(7, 0, bias_bank[1])
+        add_bias_vector(7, 0, bias_bank[0])
         store(7, 0)
         y_times_d(7, 1)
         store(6, 1)
-        add_bias_vector(7, 1, bias_bank[1])
+        add_bias_vector(7, 1, bias_bank[0])
         store(7, 1)

@@ -123,12 +123,12 @@ def tile_modulatedlinear_kernel(tc, x, modulation, weight, bias, mod_w, mod_b, o
             m_bank[k] = word_transposes(m_rows[k], tag, bufs)
 
         def mod_copy(k, copy):
-            if k % 2 == 0:
+            if k // 2 not in m_op:
                 m_op[k // 2] = operand(work, "m", 2)
             copy_out(copy, m_bank[k], values(m_op[k // 2], k % 2))
 
-        def stage1(g, j):
-            s1_bank[g, j] = psum.tile([P, D], S1_DTYPE, tag="s1", bufs=2, name="s1")
+        def stage1(g, j, tag="s1"):
+            s1_bank[g, j] = psum.tile([P, D], S1_DTYPE, tag=tag, bufs=2, name="s1")
             matmul_mx(s1_bank[g, j], mw, P * j, m_op[g])
 
         def add_mod_b(g, j, on_vector=False):
@@ -149,7 +149,7 @@ def tile_modulatedlinear_kernel(tc, x, modulation, weight, bias, mod_w, mod_b, o
             return s_sb[u // 2][:, :, UNIT * (u % 2):UNIT * (u % 2 + 1)]
 
         def s_times_s(u):
-            a_op[u] = operand(work, "a", 2)
+            a_op[u] = operand(work, "a", 4)
             nc.scalar.activation(out=values(a_op[u], 1).rearrange("p (c i j) -> p c j i", i=RUN, j=4),
                                  in_=s_of(u).rearrange("p j (c i) -> p c j i", i=RUN), func=ACT.Square)
 
@@ -167,11 +167,11 @@ def tile_modulatedlinear_kernel(tc, x, modulation, weight, bias, mod_w, mod_b, o
             matmul_mx(q_bank[u, c], a_op[u], UNIT + P * c, w2)
 
         def demod(u, c):
-            d_sb[u, c] = work.tile([P, D], F32, tag="d", name="d", bufs=4)
+            d_sb[u, c] = work.tile([P, D], F32, tag="d", name="d", bufs=16)
             nc.scalar.activation(out=d_sb[u, c][:], in_=q_bank[u, c][:], func=ACT.Abs_reciprocal_sqrt, bias=EPS, scale=1.0)
 
         def y_times_d(u, c):
-            yd_sb[u, c] = work.tile([P, D], F32, tag="yd", name="yd", bufs=6)
+            yd_sb[u, c] = work.tile([P, D], F32, tag="yd", name="yd", bufs=16)
             nc.vector.tensor_tensor(out=yd_sb[u, c][:], in0=y_bank[u, c][:], in1=d_sb[u, c][:], op=ALU.mult)
 
         def spread_bias(tag, bufs):
@@ -180,11 +180,11 @@ def tile_modulatedlinear_kernel(tc, x, modulation, weight, bias, mod_w, mod_b, o
             bias_bank.append(bank)
 
         def add_bias_gpsimd(u, c):
-            res_sb[u, c] = work.tile([P, D], F32, tag="res", name="res", bufs=8)
+            res_sb[u, c] = work.tile([P, D], F32, tag="res", name="res", bufs=16)
             nc.gpsimd.tensor_tensor(out=res_sb[u, c][:], in0=yd_sb[u, c][:], in1=bias_bf[:], op=ALU.add)
 
         def add_bias_vector(u, c, bias_tile):
-            res_sb[u, c] = work.tile([P, D], F32, tag="res", name="res", bufs=8)
+            res_sb[u, c] = work.tile([P, D], F32, tag="res", name="res", bufs=16)
             nc.vector.tensor_tensor(out=res_sb[u, c][:], in0=yd_sb[u, c][:], in1=bias_tile[:], op=ALU.add)
 
         def store(u, c):
@@ -192,9 +192,8 @@ def tile_modulatedlinear_kernel(tc, x, modulation, weight, bias, mod_w, mod_b, o
 
         mod_transposes(0, "y", 2)
         mod_transposes(1, "q", 2)
-        idle_matmul()
         mw_bank = [word_transposes(mw_rows[0], "y", 2), word_transposes(mw_rows[1], "q", 2)]
-        w_bank = [word_transposes(w_rows[0], "tm")]
+        idle_matmul()
         mod_copy(0, nc.scalar.copy)
         mod_copy(1, nc.vector.tensor_copy)
         copy_out(nc.scalar.copy, mw_bank[0], values(mw, 0))
@@ -204,22 +203,17 @@ def tile_modulatedlinear_kernel(tc, x, modulation, weight, bias, mod_w, mod_b, o
         copy_out(nc.scalar.copy, mw_bank[1], values(mw, 1))
         stage1(0, 0)
         stage1(0, 1)
-        w_bank.append(word_transposes(w_rows[1], "y", 2))
         quantize(mw, UNIT, D)
-        copy_out(nc.scalar.copy, w_bank[0], values(w, 0))
+        stage1(0, 2, "q")
+        stage1(0, 3, "y")
         add_mod_b(0, 0)
         add_mod_b(0, 1, on_vector=True)
-        stage1(0, 2)
-        stage1(0, 3)
         x_transposes(0)
-        copy_out(nc.scalar.copy, w_bank[1], values(w, 1))
-        quantize(w, 0, UNIT)
-        quantize(w, UNIT, D)
         add_mod_b(0, 2)
         add_mod_b(0, 3, on_vector=True)
         mod_transposes(2, "q", 2)
         mod_transposes(3, "y", 2)
-        mod_transposes(4)
+        w_bank = [word_transposes(w_rows[0], "tm"), word_transposes(w_rows[1], "y", 2)]
 
         for u in range(UNITS):
             g = u // 2
@@ -228,13 +222,18 @@ def tile_modulatedlinear_kernel(tc, x, modulation, weight, bias, mod_w, mod_b, o
                 x_times_s(0)
                 mod_copy(2, nc.scalar.copy)
                 mod_copy(3, nc.vector.tensor_copy)
-                nc.scalar.activation(out=values(w2, 0), in_=values(w, 0), func=ACT.Square)
-                nc.vector.tensor_tensor(out=values(w2, 1), in0=values(w, 1), in1=values(w, 1), op=ALU.mult)
                 quantize(m_op[1], 0, D)
-                quantize(w2, 0, D)
+                copy_out(nc.scalar.copy, w_bank[0], values(w, 0))
+                copy_out(nc.scalar.copy, w_bank[1], values(w, 1))
                 x_transposes(1)
                 stage1(1, 0)
                 stage1(1, 1)
+                mod_transposes(4)
+                quantize(w, 0, UNIT)
+                quantize(w, UNIT, D)
+                nc.scalar.activation(out=values(w2, 0), in_=values(w, 0), func=ACT.Square)
+                nc.vector.tensor_tensor(out=values(w2, 1), in0=values(w, 1), in1=values(w, 1), op=ALU.mult)
+                quantize(w2, 0, D)
                 add_mod_b(1, 0)
                 add_mod_b(1, 1)
                 quantize(a_op[0], 0, D)

@@ -187,8 +187,8 @@ def tile_modulatedlinear_kernel(tc, x, modulation, weight, bias, mod_w, mod_b, o
             res_sb[u, c] = work.tile([P, D], F32, tag="res", name="res", bufs=16)
             nc.vector.tensor_tensor(out=res_sb[u, c][:], in0=yd_sb[u, c][:], in1=bias_tile[:], op=ALU.add)
 
-        def store(u, c):
-            nc.sync.dma_start(out=unit_view(out, u)[:, c, :], in_=res_sb[u, c][:])
+        def store(u, c, queue=nc.sync):
+            queue.dma_start(out=unit_view(out, u)[:, c, :], in_=res_sb[u, c][:])
 
         mod_transposes(0, "y", 2)
         mod_transposes(1, "q", 2)
@@ -233,10 +233,10 @@ def tile_modulatedlinear_kernel(tc, x, modulation, weight, bias, mod_w, mod_b, o
                 quantize(w, UNIT, D)
                 nc.scalar.activation(out=values(w2, 0), in_=values(w, 0), func=ACT.Square)
                 nc.vector.tensor_tensor(out=values(w2, 1), in0=values(w, 1), in1=values(w, 1), op=ALU.mult)
-                quantize(w2, 0, D)
                 add_mod_b(1, 0)
                 add_mod_b(1, 1)
                 quantize(a_op[0], 0, D)
+                quantize(w2, 0, D)
                 stage3(0, 0)
                 stage3(0, 1)
                 continue
@@ -291,9 +291,9 @@ def tile_modulatedlinear_kernel(tc, x, modulation, weight, bias, mod_w, mod_b, o
         demod(7, 0)
         demod(7, 1)
         y_times_d(7, 0)
+        y_times_d(7, 1)
         add_bias_vector(7, 0, bias_bank[0])
         store(7, 0)
-        y_times_d(7, 1)
-        store(6, 1)
         add_bias_vector(7, 1, bias_bank[0])
         store(7, 1)
+        store(6, 1, nc.scalar)

@@ -271,10 +271,13 @@ def tile_modulatedlinear_kernel(tc, x, modulation, weight, bias, mod_w, mod_b, o
                 store(u - 2, 1)
             stage2(u - 1, 1)
             demod(u - 1, 0)
-            demod(u - 1, 1)
+            if u % 2 == 0:
+                demod(u - 1, 1)
             if g + 1 < CHUNKS:
                 add_mod_b(g + 1, 2 * (u % 2))
                 add_mod_b(g + 1, 2 * (u % 2) + 1)
+            if u % 2 == 1:
+                demod(u - 1, 1)
             quantize(a_op[u], 0, D)
             stage3(u, 0)
             stage3(u, 1)

@@ -18,6 +18,7 @@ UNITS = 8
 UNIT = 256
 RUN = 4
 EPS = 1e-8
+X_MATMUL = 8
 FLOPS = 3 * 2 * CHUNKS * D * D * D
 S1_DTYPE = BF16
 
@@ -58,12 +59,13 @@ def tile_modulatedlinear_kernel(tc, x, modulation, weight, bias, mod_w, mod_b, o
         zeros = const.tile([P, UNIT], F32, name="zeros")
         nc.vector.memset(zeros[:], 0.0)
 
-        def idle_matmul():
-            idle_bank = psum.tile([P, UNIT], F32, tag="s1", bufs=2, name="idle_bank")
-            nc.tensor.matmul(out=idle_bank[:], lhsT=zeros[:, 0:P], rhs=zeros[:], start=True, stop=True)
+        def idle_matmul(n=UNIT, tag="s1"):
+            idle_bank = psum.tile([P, UNIT], F32, tag=tag, bufs=2, name="idle_bank")
+            nc.tensor.matmul(out=idle_bank[:, 0:n], lhsT=zeros[:, 0:P], rhs=zeros[:, 0:n], start=True, stop=True)
 
-        for i in range(3):
-            idle_matmul()
+        idle_matmul(256, "s1")
+        idle_matmul(256, "s1")
+        idle_matmul(128, "s1")
 
         mw_view = mod_w.rearrange("(r c) k -> r c k", c=4)
         w_view = weight.rearrange("(c r) k -> r c k", c=4)
@@ -71,8 +73,8 @@ def tile_modulatedlinear_kernel(tc, x, modulation, weight, bias, mod_w, mod_b, o
         m_rows[0] = load(unit_view(modulation, 0), "m0")
         m_rows[1] = load(unit_view(modulation, 1), "m1")
         mw_rows = [load(mw_view[:, 0:2, :], "mw0"), load(mw_view[:, 2:4, :], "mw1")]
-        w_rows = [load(w_view[:, 0:2, :], "w0"), load(w_view[:, 2:4, :], "w1")]
         x_rows[0] = load(unit_view(x, 0), "x0")
+        w_rows = [load(w_view[:, 0:2, :], "w0"), load(w_view[:, 2:4, :], "w1")]
         m_rows[2] = load(unit_view(modulation, 2), "m2")
         m_rows[3] = load(unit_view(modulation, 3), "m3")
         x_rows[1] = load(unit_view(x, 1), "x1")
@@ -143,7 +145,10 @@ def tile_modulatedlinear_kernel(tc, x, modulation, weight, bias, mod_w, mod_b, o
             x_bank[u] = psum.tile([P, 4, UNIT], BF16, tag="tx", bufs=1, name="t_x")
             for c in range(2):
                 for j in range(4):
-                    nc.tensor.matmul(out=x_bank[u][:, j, c * P:(c + 1) * P], lhsT=x_rows[u][:, c, j:D:4], rhs=ident_bf[:], start=True, stop=True)
+                    if u < X_MATMUL:
+                        nc.tensor.matmul(out=x_bank[u][:, j, c * P:(c + 1) * P], lhsT=x_rows[u][:, c, j:D:4], rhs=ident_bf[:], start=True, stop=True)
+                    else:
+                        nc.tensor.transpose(x_bank[u][:, j, c * P:(c + 1) * P], x_rows[u][:, c, j:D:4], ident_bf[:])
 
         def s_of(u):
             return s_sb[u // 2][:, :, UNIT * (u % 2):UNIT * (u % 2 + 1)]
@@ -152,6 +157,13 @@ def tile_modulatedlinear_kernel(tc, x, modulation, weight, bias, mod_w, mod_b, o
             a_op[u] = operand(work, "a", 4)
             nc.scalar.activation(out=values(a_op[u], 1).rearrange("p (c i j) -> p c j i", i=RUN, j=4),
                                  in_=s_of(u).rearrange("p j (c i) -> p c j i", i=RUN), func=ACT.Square)
+
+        def s_times_s_gpsimd(u):
+            a_op[u] = operand(work, "a", 4)
+            for c in range(2):
+                lo = slice(P * c, P * (c + 1))
+                s = s_of(u)[:, :, lo].rearrange("p j (c i) -> p c j i", i=RUN)
+                nc.gpsimd.tensor_tensor(out=values(a_op[u], 1)[:, 4 * P * c:4 * P * (c + 1)].rearrange("p (c i j) -> p c j i", i=RUN, j=4), in0=s, in1=s, op=ALU.mult)
 
         def x_times_s(u):
             nc.vector.tensor_tensor(out=values(a_op[u], 0).rearrange("p (c i j) -> p c j i", i=RUN, j=4),
@@ -192,8 +204,9 @@ def tile_modulatedlinear_kernel(tc, x, modulation, weight, bias, mod_w, mod_b, o
 
         mod_transposes(0, "y", 2)
         mod_transposes(1, "q", 2)
-        mw_bank = [word_transposes(mw_rows[0], "y", 2), word_transposes(mw_rows[1], "q", 2)]
-        idle_matmul()
+        mw_bank = [word_transposes(mw_rows[0], "y", 2)]
+        mw_bank.append(word_transposes(mw_rows[1], "q", 2))
+        x_transposes(0)
         mod_copy(0, nc.scalar.copy)
         mod_copy(1, nc.vector.tensor_copy)
         copy_out(nc.scalar.copy, mw_bank[0], values(mw, 0))
@@ -208,47 +221,60 @@ def tile_modulatedlinear_kernel(tc, x, modulation, weight, bias, mod_w, mod_b, o
         stage1(0, 3, "y")
         add_mod_b(0, 0)
         add_mod_b(0, 1, on_vector=True)
-        x_transposes(0)
         add_mod_b(0, 2)
         add_mod_b(0, 3, on_vector=True)
         mod_transposes(2, "q", 2)
         mod_transposes(3, "y", 2)
         w_bank = [word_transposes(w_rows[0], "tm"), word_transposes(w_rows[1], "y", 2)]
 
-        for u in range(UNITS):
+        s_times_s(0)
+        x_times_s(0)
+        s_times_s_gpsimd(1)
+        mod_copy(3, nc.vector.tensor_copy)
+        mod_copy(2, nc.scalar.copy)
+        copy_out(nc.vector.tensor_copy, w_bank[0], values(w, 0))
+        copy_out(nc.scalar.copy, w_bank[1], values(w, 1))
+        x_transposes(1)
+        mod_transposes(4)
+        quantize(m_op[1], 0, D)
+        quantize(w, 0, UNIT)
+        mod_copy(4, nc.scalar.copy)
+        stage1(1, 0)
+        stage1(1, 1)
+        nc.vector.tensor_tensor(out=values(w2, 0), in0=values(w, 0), in1=values(w, 0), op=ALU.mult)
+        quantize(w, UNIT, D)
+        nc.vector.tensor_tensor(out=values(w2, 1), in0=values(w, 1), in1=values(w, 1), op=ALU.mult)
+        quantize(a_op[0], 0, D)
+        add_mod_b(1, 0)
+        add_mod_b(1, 1)
+        mod_transposes(5, "y", 2)
+        stage1(1, 2)
+        stage1(1, 3)
+        quantize(w2, 0, D)
+        stage3(0, 0)
+        stage3(0, 1)
+        add_mod_b(1, 2)
+        add_mod_b(1, 3)
+        x_times_s(1)
+        stage2(0, 0)
+        x_transposes(2)
+        mod_copy(5, nc.scalar.copy)
+        demod(0, 0)
+        demod(0, 1)
+        quantize(a_op[1], 0, D)
+        mod_transposes(6)
+        stage3(1, 0)
+        stage3(1, 1)
+        quantize(m_op[2], 0, D)
+        stage2(0, 1)
+
+        for u in range(2, UNITS):
             g = u // 2
-            if u == 0:
-                s_times_s(0)
-                x_times_s(0)
-                mod_copy(2, nc.scalar.copy)
-                mod_copy(3, nc.vector.tensor_copy)
-                quantize(m_op[1], 0, D)
-                copy_out(nc.scalar.copy, w_bank[0], values(w, 0))
-                copy_out(nc.scalar.copy, w_bank[1], values(w, 1))
-                x_transposes(1)
-                stage1(1, 0)
-                stage1(1, 1)
-                mod_transposes(4)
-                quantize(w, 0, UNIT)
-                quantize(w, UNIT, D)
-                nc.scalar.activation(out=values(w2, 0), in_=values(w, 0), func=ACT.Square)
-                nc.vector.tensor_tensor(out=values(w2, 1), in0=values(w, 1), in1=values(w, 1), op=ALU.mult)
-                add_mod_b(1, 0)
-                add_mod_b(1, 1)
-                quantize(a_op[0], 0, D)
-                quantize(w2, 0, D)
-                stage3(0, 0)
-                stage3(0, 1)
-                continue
-            if u == 1:
-                mod_copy(4, nc.vector.tensor_copy)
-                mod_transposes(5)
             if u == 4:
                 spread_bias("tm", 1)
-            if u >= 2:
-                y_times_d(u - 2, 0)
-                add_bias_gpsimd(u - 2, 0)
-                store(u - 2, 0)
+            y_times_d(u - 2, 0)
+            add_bias_gpsimd(u - 2, 0)
+            store(u - 2, 0)
             stage2(u - 1, 0)
             if g + 1 < CHUNKS:
                 stage1(g + 1, 2 * (u % 2))
@@ -257,18 +283,17 @@ def tile_modulatedlinear_kernel(tc, x, modulation, weight, bias, mod_w, mod_b, o
                 mod_copy(7, nc.vector.tensor_copy)
             s_times_s(u)
             x_times_s(u)
-            if u <= 2:
-                mod_copy(u + 4, nc.vector.tensor_copy)
+            if u == 2:
+                mod_copy(6, nc.vector.tensor_copy)
             if u == 3:
                 quantize(m_op[3], 0, D)
             if u + 1 < UNITS:
                 x_transposes(u + 1)
-            if u == 1 or u == 2:
+            if u == 2:
                 mod_transposes(u + 5)
-            if u >= 2:
-                y_times_d(u - 2, 1)
-                add_bias_gpsimd(u - 2, 1)
-                store(u - 2, 1)
+            y_times_d(u - 2, 1)
+            add_bias_gpsimd(u - 2, 1)
+            store(u - 2, 1)
             stage2(u - 1, 1)
             demod(u - 1, 0)
             if u % 2 == 0:
@@ -281,22 +306,20 @@ def tile_modulatedlinear_kernel(tc, x, modulation, weight, bias, mod_w, mod_b, o
             quantize(a_op[u], 0, D)
             stage3(u, 0)
             stage3(u, 1)
-            if u == 1:
-                quantize(m_op[2], 0, D)
 
         y_times_d(6, 0)
-        add_bias_gpsimd(6, 0)
-        store(6, 0)
         stage2(7, 0)
         y_times_d(6, 1)
         add_bias_gpsimd(6, 1)
         stage2(7, 1)
         demod(7, 0)
         demod(7, 1)
+        add_bias_vector(6, 0, bias_bank[0])
+        store(6, 0)
         y_times_d(7, 0)
+        add_bias_gpsimd(7, 0)
+        store(6, 1)
         y_times_d(7, 1)
-        add_bias_vector(7, 0, bias_bank[0])
-        store(7, 0)
         add_bias_vector(7, 1, bias_bank[0])
         store(7, 1)
-        store(6, 1, nc.scalar)
+        store(7, 0, nc.scalar)

@@ -319,7 +319,12 @@ def tile_modulatedlinear_kernel(tc, x, modulation, weight, bias, mod_w, mod_b, o
         y_times_d(7, 0)
         add_bias_gpsimd(7, 0)
         store(6, 1)
-        y_times_d(7, 1)
-        add_bias_vector(7, 1, bias_bank[0])
-        store(7, 1)
+        yd_sb[7, 1] = work.tile([P, D], F32, tag="yd", name="yd", bufs=16)
+        res_sb[7, 1] = work.tile([P, D], F32, tag="res", name="res", bufs=16)
+        halves = [slice(0, D // 2), slice(D // 2, D)]
+        for n in halves:
+            nc.vector.tensor_tensor(out=yd_sb[7, 1][:, n], in0=y_bank[7, 1][:, n], in1=d_sb[7, 1][:, n], op=ALU.mult)
+        for n in halves:
+            nc.vector.tensor_tensor(out=res_sb[7, 1][:, n], in0=yd_sb[7, 1][:, n], in1=bias_bank[0][:, n], op=ALU.add)
+            nc.sync.dma_start(out=unit_view(out, 7)[:, 1, n], in_=res_sb[7, 1][:, n])
         store(7, 0, nc.scalar)

@@ -183,8 +183,10 @@ def tile_modulatedlinear_kernel(tc, x, modulation, weight, bias, mod_w, mod_b, o
             nc.scalar.activation(out=d_sb[u, c][:], in_=q_bank[u, c][:], func=ACT.Abs_reciprocal_sqrt, bias=EPS, scale=1.0)
 
         def y_times_d(u, c):
-            yd_sb[u, c] = work.tile([P, D], F32, tag="yd", name="yd", bufs=16)
-            nc.vector.tensor_tensor(out=yd_sb[u, c][:], in0=y_bank[u, c][:], in1=d_sb[u, c][:], op=ALU.mult)
+            if c == 0:
+                yd_sb[u] = work.tile([P, 2, D], F32, tag="yd", name="yd", bufs=8)
+                res_sb[u] = work.tile([P, 2, D], F32, tag="res", name="res", bufs=8)
+            nc.vector.tensor_tensor(out=yd_sb[u][:, c, :], in0=y_bank[u, c][:], in1=d_sb[u, c][:], op=ALU.mult)
 
         def spread_bias(tag, bufs):
             bank = psum.tile([P, D], F32, tag=tag, bufs=bufs, name="bias_bank")
@@ -192,15 +194,19 @@ def tile_modulatedlinear_kernel(tc, x, modulation, weight, bias, mod_w, mod_b, o
             bias_bank.append(bank)
 
         def add_bias_gpsimd(u, c):
-            res_sb[u, c] = work.tile([P, D], F32, tag="res", name="res", bufs=16)
-            nc.gpsimd.tensor_tensor(out=res_sb[u, c][:], in0=yd_sb[u, c][:], in1=bias_bf[:], op=ALU.add)
+            nc.gpsimd.tensor_tensor(out=res_sb[u][:, c, :], in0=yd_sb[u][:, c, :], in1=bias_bf[:], op=ALU.add)
+
+        def add_bias_gpsimd_unit(u):
+            nc.gpsimd.tensor_tensor(out=res_sb[u][:], in0=yd_sb[u][:], in1=bias_bf[:].unsqueeze(1).to_broadcast([P, 2, D]), op=ALU.add)
 
         def add_bias_vector(u, c, bias_tile):
-            res_sb[u, c] = work.tile([P, D], F32, tag="res", name="res", bufs=16)
-            nc.vector.tensor_tensor(out=res_sb[u, c][:], in0=yd_sb[u, c][:], in1=bias_tile[:], op=ALU.add)
+            nc.vector.tensor_tensor(out=res_sb[u][:, c, :], in0=yd_sb[u][:, c, :], in1=bias_tile[:], op=ALU.add)
 
         def store(u, c, queue=nc.sync):
-            queue.dma_start(out=unit_view(out, u)[:, c, :], in_=res_sb[u, c][:])
+            queue.dma_start(out=unit_view(out, u)[:, c, :], in_=res_sb[u][:, c, :])
+
+        def store_unit(u):
+            nc.sync.dma_start(out=unit_view(out, u), in_=res_sb[u][:])
 
         mod_transposes(0, "y", 2)
         mod_transposes(1, "q", 2)
@@ -273,8 +279,6 @@ def tile_modulatedlinear_kernel(tc, x, modulation, weight, bias, mod_w, mod_b, o
             if u == 4:
                 spread_bias("tm", 1)
             y_times_d(u - 2, 0)
-            add_bias_gpsimd(u - 2, 0)
-            store(u - 2, 0)
             stage2(u - 1, 0)
             if g + 1 < CHUNKS:
                 stage1(g + 1, 2 * (u % 2))
@@ -292,8 +296,8 @@ def tile_modulatedlinear_kernel(tc, x, modulation, weight, bias, mod_w, mod_b, o
             if u == 2:
                 mod_transposes(u + 5)
             y_times_d(u - 2, 1)
-            add_bias_gpsimd(u - 2, 1)
-            store(u - 2, 1)
+            add_bias_gpsimd_unit(u - 2)
+            store_unit(u - 2)
             stage2(u - 1, 1)
             demod(u - 1, 0)
             if u % 2 == 0:
@@ -319,12 +323,10 @@ def tile_modulatedlinear_kernel(tc, x, modulation, weight, bias, mod_w, mod_b, o
         y_times_d(7, 0)
         add_bias_gpsimd(7, 0)
         store(6, 1)
-        yd_sb[7, 1] = work.tile([P, D], F32, tag="yd", name="yd", bufs=16)
-        res_sb[7, 1] = work.tile([P, D], F32, tag="res", name="res", bufs=16)
         halves = [slice(0, D // 2), slice(D // 2, D)]
         for n in halves:
-            nc.vector.tensor_tensor(out=yd_sb[7, 1][:, n], in0=y_bank[7, 1][:, n], in1=d_sb[7, 1][:, n], op=ALU.mult)
+            nc.vector.tensor_tensor(out=yd_sb[7][:, 1, n], in0=y_bank[7, 1][:, n], in1=d_sb[7, 1][:, n], op=ALU.mult)
         for n in halves:
-            nc.vector.tensor_tensor(out=res_sb[7, 1][:, n], in0=yd_sb[7, 1][:, n], in1=bias_bank[0][:, n], op=ALU.add)
-            nc.sync.dma_start(out=unit_view(out, 7)[:, 1, n], in_=res_sb[7, 1][:, n])
+            nc.vector.tensor_tensor(out=res_sb[7][:, 1, n], in0=yd_sb[7][:, 1, n], in1=bias_bank[0][:, n], op=ALU.add)
+            nc.sync.dma_start(out=unit_view(out, 7)[:, 1, n], in_=res_sb[7][:, 1, n])
         store(7, 0, nc.scalar)

@@ -18,7 +18,6 @@ UNITS = 8
 UNIT = 256
 RUN = 4
 EPS = 1e-8
-X_MATMUL = 8
 FLOPS = 3 * 2 * CHUNKS * D * D * D
 S1_DTYPE = BF16
 
@@ -142,13 +141,12 @@ def tile_modulatedlinear_kernel(tc, x, modulation, weight, bias, mod_w, mod_b, o
                 nc.scalar.activation(out=s_sb[g][:, j, :], in_=s1_bank[g, j][:], func=ACT.Identity, bias=modb[:, j:j + 1], scale=1.0)
 
         def x_transposes(u):
-            x_bank[u] = psum.tile([P, 4, UNIT], BF16, tag="tx", bufs=1, name="t_x")
+            bank = psum.tile([P, UNIT, 2], F32, tag="tx", bufs=1, name="t_x")
             for c in range(2):
-                for j in range(4):
-                    if u < X_MATMUL:
-                        nc.tensor.matmul(out=x_bank[u][:, j, c * P:(c + 1) * P], lhsT=x_rows[u][:, c, j:D:4], rhs=ident_bf[:], start=True, stop=True)
-                    else:
-                        nc.tensor.transpose(x_bank[u][:, j, c * P:(c + 1) * P], x_rows[u][:, c, j:D:4], ident_bf[:])
+                words = x_rows[u][:, c, :].bitcast(F32)
+                for h in range(2):
+                    nc.tensor.transpose(bank[:, c * P:(c + 1) * P, h], words[:, h:UNIT:2], ident[:])
+            x_bank[u] = bank[:].rearrange("p n h -> p (n h)").bitcast(BF16)
 
         def s_of(u):
             return s_sb[u // 2][:, :, UNIT * (u % 2):UNIT * (u % 2 + 1)]
@@ -168,7 +166,7 @@ def tile_modulatedlinear_kernel(tc, x, modulation, weight, bias, mod_w, mod_b, o
         def x_times_s(u):
             nc.vector.tensor_tensor(out=values(a_op[u], 0).rearrange("p (c i j) -> p c j i", i=RUN, j=4),
                                     in0=s_of(u).rearrange("p j (c i) -> p c j i", i=RUN),
-                                    in1=x_bank[u][:].rearrange("p j (c i) -> p c j i", i=RUN), op=ALU.mult)
+                                    in1=x_bank[u].rearrange("p (c i j) -> p c j i", i=RUN, j=4), op=ALU.mult)
 
         def stage2(u, c):
             y_bank[u, c] = psum.tile([P, D], F32, tag="y", bufs=2, name="y")
@@ -213,6 +211,7 @@ def tile_modulatedlinear_kernel(tc, x, modulation, weight, bias, mod_w, mod_b, o
         mw_bank = [word_transposes(mw_rows[0], "y", 2)]
         mw_bank.append(word_transposes(mw_rows[1], "q", 2))
         x_transposes(0)
+        idle_matmul(256, "s1")
         mod_copy(0, nc.scalar.copy)
         mod_copy(1, nc.vector.tensor_copy)
         copy_out(nc.scalar.copy, mw_bank[0], values(mw, 0))
@@ -241,6 +240,7 @@ def tile_modulatedlinear_kernel(tc, x, modulation, weight, bias, mod_w, mod_b, o
         copy_out(nc.vector.tensor_copy, w_bank[0], values(w, 0))
         copy_out(nc.scalar.copy, w_bank[1], values(w, 1))
         x_transposes(1)
+        idle_matmul(256, "q")
         mod_transposes(4)
         quantize(m_op[1], 0, D)
         quantize(w, 0, UNIT)

@@ -64,7 +64,6 @@ def tile_modulatedlinear_kernel(tc, x, modulation, weight, bias, mod_w, mod_b, o
 
         idle_matmul(256, "s1")
         idle_matmul(256, "s1")
-        idle_matmul(128, "s1")
 
         mw_view = mod_w.rearrange("(r c) k -> r c k", c=4)
         w_view = weight.rearrange("(c r) k -> r c k", c=4)
@@ -208,6 +207,7 @@ def tile_modulatedlinear_kernel(tc, x, modulation, weight, bias, mod_w, mod_b, o
 
         mod_transposes(0, "y", 2)
         mod_transposes(1, "q", 2)
+        idle_matmul(256, "s1")
         mw_bank = [word_transposes(mw_rows[0], "y", 2)]
         mw_bank.append(word_transposes(mw_rows[1], "q", 2))
         x_transposes(0)
@@ -230,6 +230,7 @@ def tile_modulatedlinear_kernel(tc, x, modulation, weight, bias, mod_w, mod_b, o
         add_mod_b(0, 3, on_vector=True)
         mod_transposes(2, "q", 2)
         mod_transposes(3, "y", 2)
+        idle_matmul(256, "q")
         w_bank = [word_transposes(w_rows[0], "tm"), word_transposes(w_rows[1], "y", 2)]
 
         s_times_s(0)
@@ -253,6 +254,7 @@ def tile_modulatedlinear_kernel(tc, x, modulation, weight, bias, mod_w, mod_b, o
         quantize(a_op[0], 0, D)
         add_mod_b(1, 0)
         add_mod_b(1, 1)
+        idle_matmul(256, "q")
         mod_transposes(5, "y", 2)
         stage1(1, 2)
         stage1(1, 3)
@@ -279,6 +281,9 @@ def tile_modulatedlinear_kernel(tc, x, modulation, weight, bias, mod_w, mod_b, o
             if u == 4:
                 spread_bias("tm", 1)
             y_times_d(u - 2, 0)
+            if u - 2 >= 5:
+                add_bias_gpsimd(u - 2, 0)
+                store(u - 2, 0)
             stage2(u - 1, 0)
             if g + 1 < CHUNKS:
                 stage1(g + 1, 2 * (u % 2))
@@ -296,8 +301,12 @@ def tile_modulatedlinear_kernel(tc, x, modulation, weight, bias, mod_w, mod_b, o
             if u == 2:
                 mod_transposes(u + 5)
             y_times_d(u - 2, 1)
-            add_bias_gpsimd_unit(u - 2)
-            store_unit(u - 2)
+            if u - 2 >= 5:
+                add_bias_gpsimd(u - 2, 1)
+                store(u - 2, 1)
+            else:
+                add_bias_gpsimd_unit(u - 2)
+                store_unit(u - 2)
             stage2(u - 1, 1)
             demod(u - 1, 0)
             if u % 2 == 0:
@@ -321,12 +330,12 @@ def tile_modulatedlinear_kernel(tc, x, modulation, weight, bias, mod_w, mod_b, o
         add_bias_vector(6, 0, bias_bank[0])
         store(6, 0)
         y_times_d(7, 0)
-        add_bias_gpsimd(7, 0)
-        store(6, 1)
         halves = [slice(0, D // 2), slice(D // 2, D)]
         for n in halves:
             nc.vector.tensor_tensor(out=yd_sb[7][:, 1, n], in0=y_bank[7, 1][:, n], in1=d_sb[7, 1][:, n], op=ALU.mult)
+        add_bias_vector(7, 0, bias_bank[0])
+        store(7, 0)
         for n in halves:
             nc.vector.tensor_tensor(out=res_sb[7][:, 1, n], in0=yd_sb[7][:, 1, n], in1=bias_bank[0][:, n], op=ALU.add)
             nc.sync.dma_start(out=unit_view(out, 7)[:, 1, n], in_=res_sb[7][:, 1, n])
-        store(7, 0, nc.scalar)
+        store(6, 1, nc.scalar)

@@ -157,10 +157,8 @@ def tile_modulatedlinear_kernel(tc, x, modulation, weight, bias, mod_w, mod_b, o
 
         def s_times_s_gpsimd(u):
             a_op[u] = operand(work, "a", 4)
-            for c in range(2):
-                lo = slice(P * c, P * (c + 1))
-                s = s_of(u)[:, :, lo].rearrange("p j (c i) -> p c j i", i=RUN)
-                nc.gpsimd.tensor_tensor(out=values(a_op[u], 1)[:, 4 * P * c:4 * P * (c + 1)].rearrange("p (c i j) -> p c j i", i=RUN, j=4), in0=s, in1=s, op=ALU.mult)
+            s = s_of(u).rearrange("p j n -> p n j")
+            nc.gpsimd.tensor_tensor(out=values(a_op[u], 1).rearrange("p (n j) -> p n j", j=4), in0=s, in1=s, op=ALU.mult)
 
         def x_times_s(u):
             nc.vector.tensor_tensor(out=values(a_op[u], 0).rearrange("p (c i j) -> p c j i", i=RUN, j=4),

@@ -46,14 +46,12 @@ def tile_modulatedlinear_kernel(tc, x, modulation, weight, bias, mod_w, mod_b, o
         one = const.tile([P, 1], F32, name="one")
         nc.vector.memset(one[:], 1.0)
         warm = const.tile([P, 1], F32, name="warm")
-        modb_bf = const.tile([P, 4], BF16, name="modb_bf")
-        nc.scalar.dma_start(out=modb_bf[:], in_=mod_b.rearrange("(p j) -> p j", j=4))
+        modb = const.tile([P, 4], BF16, name="modb")
         bias_row = const.tile([P, D], BF16, name="bias_row")
         nc.gpsimd.memset(bias_row[:], 0.0)
         nc.scalar.activation(out=warm[:], in_=one[:], func=ACT.Abs_reciprocal_sqrt, bias=EPS, scale=1.0)
         ones = const.tile([P, P], BF16, name="ones")
         nc.gpsimd.memset(ones[:], 1.0)
-        nc.gpsimd.dma_start(out=bias_row[0:1, :], in_=bias.rearrange("(a n) -> a n", a=1))
 
         zeros = const.tile([P, UNIT], F32, name="zeros")
         nc.vector.memset(zeros[:], 0.0)
@@ -71,6 +69,7 @@ def tile_modulatedlinear_kernel(tc, x, modulation, weight, bias, mod_w, mod_b, o
         m_rows[0] = load(unit_view(modulation, 0), "m0")
         m_rows[1] = load(unit_view(modulation, 1), "m1")
         mw_rows = [load(mw_view[:, 0:2, :], "mw0"), load(mw_view[:, 2:4, :], "mw1")]
+        nc.sync.dma_start(out=modb[:], in_=mod_b.rearrange("(p j) -> p j", j=4))
         x_rows[0] = load(unit_view(x, 0), "x0")
         w_rows = [load(w_view[:, 0:2, :], "w0"), load(w_view[:, 2:4, :], "w1")]
         m_rows[2] = load(unit_view(modulation, 2), "m2")
@@ -81,11 +80,9 @@ def tile_modulatedlinear_kernel(tc, x, modulation, weight, bias, mod_w, mod_b, o
                 m_rows[u + 2] = load(unit_view(modulation, u + 2), "m%d" % (u + 2))
             x_rows[u] = load(unit_view(x, u), "x%d" % u)
 
+        nc.sync.dma_start(out=bias_row[0:1, :], in_=bias.rearrange("(a n) -> a n", a=1))
         bias_bf = const.tile([P, D], BF16, name="bias_bf")
         nc.sync.dma_start(out=bias_bf[:], in_=bias.partition_broadcast(P))
-
-        modb = const.tile([P, 4], F32, name="modb")
-        nc.vector.tensor_copy(out=modb[:], in_=modb_bf[:])
 
         def operand(pool, name, bufs):
             return (pool.tile([P, 4 * D], BF16, tag=name + "_v", name=name + "_v", bufs=bufs, align_bytes=64),
@@ -286,9 +283,9 @@ def tile_modulatedlinear_kernel(tc, x, modulation, weight, bias, mod_w, mod_b, o
             if g + 1 < CHUNKS:
                 stage1(g + 1, 2 * (u % 2))
                 stage1(g + 1, 2 * (u % 2) + 1)
-            if u == 3:
-                mod_copy(7, nc.vector.tensor_copy)
             s_times_s(u)
+            if u == 3:
+                mod_copy(7, nc.scalar.copy)
             x_times_s(u)
             if u == 2:
                 mod_copy(6, nc.vector.tensor_copy)

from contextlib import ExitStack

import concourse.mybir as mybir
from concourse.masks import make_identity

F32 = mybir.dt.float32
BF16 = mybir.dt.bfloat16
U32 = mybir.dt.uint32
U8 = mybir.dt.uint8
FP8X4 = mybir.dt.float8_e4m3fn_x4
ACT = mybir.ActivationFunctionType
ALU = mybir.AluOpType

P = 128
D = 512
CHUNKS = 4
UNITS = 8
UNIT = 256
RUN = 4
EPS = 1e-8
FLOPS = 3 * 2 * CHUNKS * D * D * D
S1_DTYPE = BF16


def tile_modulatedlinear_kernel(tc, x, modulation, weight, bias, mod_w, mod_b, out):
    nc = tc.nc
    with ExitStack() as ctx:
        const = ctx.enter_context(tc.tile_pool(name="const", bufs=1))
        rows = ctx.enter_context(tc.tile_pool(name="rows", bufs=1))
        work = ctx.enter_context(tc.tile_pool(name="work", bufs=2))
        psum = ctx.enter_context(tc.psum_pool(name="psum", bufs=1))
        ctx.enter_context(tc.manual_schedule())

        def unit_view(tensor, u):
            return tensor[u // 2].rearrange("(r c) k -> r c k", c=4)[:, 2 * (u % 2):2 * (u % 2) + 2, :]

        def load(view, name):
            t = rows.tile([P, 2, D], BF16, name=name)
            nc.sync.dma_start(out=t[:], in_=view)
            return t

        ident = const.tile([P, P], F32, name="ident")
        make_identity(nc, ident[:])
        ident_bf = const.tile([P, P], BF16, name="ident_bf")
        make_identity(nc, ident_bf[:])
        one = const.tile([P, 1], F32, name="one")
        nc.vector.memset(one[:], 1.0)
        warm = const.tile([P, 1], F32, name="warm")
        modb = const.tile([P, 4], BF16, name="modb")
        bias_row = const.tile([P, D], BF16, name="bias_row")
        nc.gpsimd.memset(bias_row[:], 0.0)
        nc.scalar.activation(out=warm[:], in_=one[:], func=ACT.Abs_reciprocal_sqrt, bias=EPS, scale=1.0)
        ones = const.tile([P, P], BF16, name="ones")
        nc.gpsimd.memset(ones[:], 1.0)

        zeros = const.tile([P, UNIT], F32, name="zeros")
        nc.vector.memset(zeros[:], 0.0)

        def idle_matmul(n=UNIT, tag="s1"):
            idle_bank = psum.tile([P, UNIT], F32, tag=tag, bufs=2, name="idle_bank")
            nc.tensor.matmul(out=idle_bank[:, 0:n], lhsT=zeros[:, 0:P], rhs=zeros[:, 0:n], start=True, stop=True)

        idle_matmul(256, "s1")
        idle_matmul(256, "s1")

        mw_view = mod_w.rearrange("(r c) k -> r c k", c=4)
        w_view = weight.rearrange("(c r) k -> r c k", c=4)
        m_rows, x_rows = {}, {}
        m_rows[0] = load(unit_view(modulation, 0), "m0")
        m_rows[1] = load(unit_view(modulation, 1), "m1")
        mw_rows = [load(mw_view[:, 0:2, :], "mw0"), load(mw_view[:, 2:4, :], "mw1")]
        nc.sync.dma_start(out=modb[:], in_=mod_b.rearrange("(p j) -> p j", j=4))
        x_rows[0] = load(unit_view(x, 0), "x0")
        w_rows = [load(w_view[:, 0:2, :], "w0"), load(w_view[:, 2:4, :], "w1")]
        m_rows[2] = load(unit_view(modulation, 2), "m2")
        m_rows[3] = load(unit_view(modulation, 3), "m3")
        x_rows[1] = load(unit_view(x, 1), "x1")
        for u in range(2, UNITS):
            if u + 2 < UNITS:
                m_rows[u + 2] = load(unit_view(modulation, u + 2), "m%d" % (u + 2))
            x_rows[u] = load(unit_view(x, u), "x%d" % u)

        nc.sync.dma_start(out=bias_row[0:1, :], in_=bias.rearrange("(a n) -> a n", a=1))
        bias_bf = const.tile([P, D], BF16, name="bias_bf")
        nc.sync.dma_start(out=bias_bf[:], in_=bias.partition_broadcast(P))

        def operand(pool, name, bufs):
            return (pool.tile([P, 4 * D], BF16, tag=name + "_v", name=name + "_v", bufs=bufs, align_bytes=64),
                    pool.tile([P, D], U32, tag=name + "_c", name=name + "_c", bufs=bufs, align_bytes=64),
                    pool.tile([P, D], U8, tag=name + "_s", name=name + "_s", bufs=bufs, align_bytes=64))

        def values(op, h):
            return op[0][:, 4 * UNIT * h:4 * UNIT * (h + 1)]

        def quantize(op, lo, hi):
            nc.vector.quantize_mx(out=op[1][:, lo:hi].bitcast(FP8X4), scales=op[2][:, lo:hi], in_=op[0][:, 4 * lo:4 * hi])

        def matmul_mx(acc, a, a0, b):
            nc.tensor.matmul_mx(out=acc[:], lhsT=a[1][:, a0:a0 + P].bitcast(FP8X4), lhsT_scale=a[2][:, a0:a0 + P],
                                rhs=b[1][:].bitcast(FP8X4), rhs_scale=b[2][:], start=True, stop=True)

        def word_transposes(src, tag, bufs=1):
            bank = psum.tile([P, 2, UNIT], F32, tag=tag, bufs=bufs, name="t_" + tag)
            for c in range(2):
                words = src[:, c, :].bitcast(F32)
                for h in range(2):
                    nc.tensor.transpose(bank[:, h, c * P:(c + 1) * P], words[:, h:UNIT:2], ident[:])
            return bank

        def copy_out(copy, bank, dst):
            copy(out=dst.bitcast(F32).rearrange("p (n h) -> p n h", h=2), in_=bank[:].rearrange("p h n -> p n h"))

        mw = operand(const, "mw", 1)
        w = operand(const, "w", 1)
        w2 = operand(const, "w2", 1)
        bias_bank = []
        m_bank, x_bank, m_op, s1_bank, s_sb, a_op, y_bank, q_bank, d_sb, yd_sb, res_sb = {}, {}, {}, {}, {}, {}, {}, {}, {}, {}, {}

        def mod_transposes(k, tag="tm", bufs=1):
            m_bank[k] = word_transposes(m_rows[k], tag, bufs)

        def mod_copy(k, copy):
            if k // 2 not in m_op:
                m_op[k // 2] = operand(work, "m", 2)
            copy_out(copy, m_bank[k], values(m_op[k // 2], k % 2))

        def stage1(g, j, tag="s1"):
            s1_bank[g, j] = psum.tile([P, D], S1_DTYPE, tag=tag, bufs=2, name="s1")
            matmul_mx(s1_bank[g, j], mw, P * j, m_op[g])

        def add_mod_b(g, j, on_vector=False):
            if j == 0:
                s_sb[g] = work.tile([P, 4, D], F32, tag="s", name="s", bufs=2)
            if on_vector:
                nc.vector.tensor_scalar(out=s_sb[g][:, j, :], in0=s1_bank[g, j][:], scalar1=modb[:, j:j + 1], scalar2=None, op0=ALU.add)
            else:
                nc.scalar.activation(out=s_sb[g][:, j, :], in_=s1_bank[g, j][:], func=ACT.Identity, bias=modb[:, j:j + 1], scale=1.0)

        def x_transposes(u):
            bank = psum.tile([P, UNIT, 2], F32, tag="tx", bufs=1, name="t_x")
            for c in range(2):
                words = x_rows[u][:, c, :].bitcast(F32)
                for h in range(2):
                    nc.tensor.transpose(bank[:, c * P:(c + 1) * P, h], words[:, h:UNIT:2], ident[:])
            x_bank[u] = bank[:].rearrange("p n h -> p (n h)").bitcast(BF16)

        def s_of(u):
            return s_sb[u // 2][:, :, UNIT * (u % 2):UNIT * (u % 2 + 1)]

        def s_times_s(u):
            a_op[u] = operand(work, "a", 4)
            nc.scalar.activation(out=values(a_op[u], 1).rearrange("p (c i j) -> p c j i", i=RUN, j=4),
                                 in_=s_of(u).rearrange("p j (c i) -> p c j i", i=RUN), func=ACT.Square)

        def s_times_s_gpsimd(u):
            a_op[u] = operand(work, "a", 4)
            s = s_of(u).rearrange("p j n -> p n j")
            nc.gpsimd.tensor_tensor(out=values(a_op[u], 1).rearrange("p (n j) -> p n j", j=4), in0=s, in1=s, op=ALU.mult)

        def x_times_s(u):
            nc.vector.tensor_tensor(out=values(a_op[u], 0).rearrange("p (c i j) -> p c j i", i=RUN, j=4),
                                    in0=s_of(u).rearrange("p j (c i) -> p c j i", i=RUN),
                                    in1=x_bank[u].rearrange("p (c i j) -> p c j i", i=RUN, j=4), op=ALU.mult)

        def stage2(u, c):
            y_bank[u, c] = psum.tile([P, D], F32, tag="y", bufs=2, name="y")
            matmul_mx(y_bank[u, c], a_op[u], P * c, w)

        def stage3(u, c):
            q_bank[u, c] = psum.tile([P, D], F32, tag="q", bufs=2, name="q")
            matmul_mx(q_bank[u, c], a_op[u], UNIT + P * c, w2)

        def demod(u, c):
            d_sb[u, c] = work.tile([P, D], F32, tag="d", name="d", bufs=16)
            nc.scalar.activation(out=d_sb[u, c][:], in_=q_bank[u, c][:], func=ACT.Abs_reciprocal_sqrt, bias=EPS, scale=1.0)

        def y_times_d(u, c):
            if c == 0:
                yd_sb[u] = work.tile([P, 2, D], F32, tag="yd", name="yd", bufs=8)
                res_sb[u] = work.tile([P, 2, D], F32, tag="res", name="res", bufs=8)
            nc.vector.tensor_tensor(out=yd_sb[u][:, c, :], in0=y_bank[u, c][:], in1=d_sb[u, c][:], op=ALU.mult)

        def spread_bias(tag, bufs):
            bank = psum.tile([P, D], F32, tag=tag, bufs=bufs, name="bias_bank")
            nc.tensor.matmul(out=bank[:], lhsT=ones[:], rhs=bias_row[:], start=True, stop=True)
            bias_bank.append(bank)

        def add_bias_gpsimd(u, c):
            nc.gpsimd.tensor_tensor(out=res_sb[u][:, c, :], in0=yd_sb[u][:, c, :], in1=bias_bf[:], op=ALU.add)

        def add_bias_gpsimd_unit(u):
            nc.gpsimd.tensor_tensor(out=res_sb[u][:], in0=yd_sb[u][:], in1=bias_bf[:].unsqueeze(1).to_broadcast([P, 2, D]), op=ALU.add)

        def add_bias_vector(u, c, bias_tile):
            nc.vector.tensor_tensor(out=res_sb[u][:, c, :], in0=yd_sb[u][:, c, :], in1=bias_tile[:], op=ALU.add)

        def store(u, c, queue=nc.sync):
            queue.dma_start(out=unit_view(out, u)[:, c, :], in_=res_sb[u][:, c, :])

        def store_unit(u):
            nc.sync.dma_start(out=unit_view(out, u), in_=res_sb[u][:])

        mod_transposes(0, "y", 2)
        mod_transposes(1, "q", 2)
        idle_matmul(256, "s1")
        mw_bank = [word_transposes(mw_rows[0], "y", 2)]
        mw_bank.append(word_transposes(mw_rows[1], "q", 2))
        x_transposes(0)
        idle_matmul(256, "s1")
        mod_copy(0, nc.scalar.copy)
        mod_copy(1, nc.vector.tensor_copy)
        copy_out(nc.scalar.copy, mw_bank[0], values(mw, 0))
        quantize(m_op[0], 0, UNIT)
        quantize(m_op[0], UNIT, D)
        quantize(mw, 0, UNIT)
        copy_out(nc.scalar.copy, mw_bank[1], values(mw, 1))
        stage1(0, 0)
        stage1(0, 1)
        quantize(mw, UNIT, D)
        stage1(0, 2, "q")
        stage1(0, 3, "y")
        add_mod_b(0, 0)
        add_mod_b(0, 1, on_vector=True)
        add_mod_b(0, 2)
        add_mod_b(0, 3, on_vector=True)
        mod_transposes(2, "q", 2)
        mod_transposes(3, "y", 2)
        idle_matmul(256, "q")
        w_bank = [word_transposes(w_rows[0], "tm"), word_transposes(w_rows[1], "y", 2)]

        s_times_s(0)
        x_times_s(0)
        s_times_s_gpsimd(1)
        mod_copy(3, nc.vector.tensor_copy)
        mod_copy(2, nc.scalar.copy)
        copy_out(nc.vector.tensor_copy, w_bank[0], values(w, 0))
        copy_out(nc.scalar.copy, w_bank[1], values(w, 1))
        x_transposes(1)
        idle_matmul(256, "q")
        mod_transposes(4)
        quantize(m_op[1], 0, D)
        quantize(w, 0, UNIT)
        mod_copy(4, nc.scalar.copy)
        stage1(1, 0)
        stage1(1, 1)
        nc.vector.tensor_tensor(out=values(w2, 0), in0=values(w, 0), in1=values(w, 0), op=ALU.mult)
        quantize(w, UNIT, D)
        nc.vector.tensor_tensor(out=values(w2, 1), in0=values(w, 1), in1=values(w, 1), op=ALU.mult)
        quantize(a_op[0], 0, D)
        add_mod_b(1, 0)
        add_mod_b(1, 1)
        idle_matmul(256, "q")
        mod_transposes(5, "y", 2)
        stage1(1, 2)
        stage1(1, 3)
        quantize(w2, 0, D)
        stage3(0, 0)
        stage3(0, 1)
        add_mod_b(1, 2)
        add_mod_b(1, 3)
        x_times_s(1)
        stage2(0, 0)
        x_transposes(2)
        mod_copy(5, nc.scalar.copy)
        demod(0, 0)
        demod(0, 1)
        quantize(a_op[1], 0, D)
        mod_transposes(6)
        stage3(1, 0)
        stage3(1, 1)
        quantize(m_op[2], 0, D)
        stage2(0, 1)

        for u in range(2, UNITS):
            g = u // 2
            if u == 4:
                spread_bias("tm", 1)
            y_times_d(u - 2, 0)
            if u - 2 >= 5:
                add_bias_gpsimd(u - 2, 0)
                store(u - 2, 0)
            stage2(u - 1, 0)
            if g + 1 < CHUNKS:
                stage1(g + 1, 2 * (u % 2))
                stage1(g + 1, 2 * (u % 2) + 1)
            s_times_s(u)
            if u == 3:
                mod_copy(7, nc.scalar.copy)
            x_times_s(u)
            if u == 2:
                mod_copy(6, nc.vector.tensor_copy)
            if u == 3:
                quantize(m_op[3], 0, D)
            if u + 1 < UNITS:
                x_transposes(u + 1)
            if u == 2:
                mod_transposes(u + 5)
            y_times_d(u - 2, 1)
            if u - 2 >= 5:
                add_bias_gpsimd(u - 2, 1)
                store(u - 2, 1)
            else:
                add_bias_gpsimd_unit(u - 2)
                store_unit(u - 2)
            stage2(u - 1, 1)
            demod(u - 1, 0)
            if u % 2 == 0:
                demod(u - 1, 1)
            if g + 1 < CHUNKS:
                add_mod_b(g + 1, 2 * (u % 2))
                add_mod_b(g + 1, 2 * (u % 2) + 1)
            if u % 2 == 1:
                demod(u - 1, 1)
            quantize(a_op[u], 0, D)
            stage3(u, 0)
            stage3(u, 1)

        y_times_d(6, 0)
        stage2(7, 0)
        y_times_d(6, 1)
        add_bias_gpsimd(6, 1)
        stage2(7, 1)
        demod(7, 0)
        demod(7, 1)
        add_bias_vector(6, 0, bias_bank[0])
        store(6, 0)
        y_times_d(7, 0)
        halves = [slice(0, D // 2), slice(D // 2, D)]
        for n in halves:
            nc.vector.tensor_tensor(out=yd_sb[7][:, 1, n], in0=y_bank[7, 1][:, n], in1=d_sb[7, 1][:, n], op=ALU.mult)
        add_bias_vector(7, 0, bias_bank[0])
        store(7, 0)
        for n in halves:
            nc.vector.tensor_tensor(out=res_sb[7][:, 1, n], in0=yd_sb[7][:, 1, n], in1=bias_bank[0][:, n], op=ALU.add)
            nc.sync.dma_start(out=unit_view(out, 7)[:, 1, n], in_=res_sb[7][:, 1, n])
        store(6, 1, nc.scalar)
